import numpy as np
import ml_dtypes


def mxq(x, axis, fmt="e4m3"):
    dtype, down = {"e4m3": (ml_dtypes.float8_e4m3fn, 7), "e5m2": (ml_dtypes.float8_e5m2, 14)}[fmt]
    v = np.moveaxis(np.asarray(x, np.float32).astype(ml_dtypes.bfloat16).astype(np.float64), axis, -1)
    blocks = v.reshape(v.shape[:-1] + (-1, 32))
    amax = np.abs(blocks).max(-1, keepdims=True)
    byte = np.maximum(np.where(amax > 0, np.frexp(amax)[1] - 1 + 127, 0) - down, 1)
    scale = np.exp2(byte - 127.0)
    codes = (blocks / scale).astype(np.float32).astype(dtype).astype(np.float64)
    return np.moveaxis((codes * scale).reshape(v.shape), -1, axis)


WIDE = False


def mx_kscale(k):
    if not WIDE:
        return np.ones(k)
    levels = np.array([10, -10, 5, -5, 0])
    a = np.random.permutation(np.resize(levels, k // 512 * 4)).reshape(k // 512, 4)
    idx = np.arange(k)
    return np.exp2(a[idx // 512, idx % 128 // 32])


BF16 = ml_dtypes.bfloat16


def bf(x):
    return np.asarray(x, np.float32).astype(BF16)


def f64(x):
    return np.asarray(x).astype(np.float64)


B, C, K, BK, BN = 16384, 512, 128, 1, 16
KEEP = 0.3


def setup_inputs():
    s = mx_kscale(C)
    x = np.random.standard_normal((B, C)) * s
    weight = np.random.uniform(-1.0, 1.0, (K, C)) * 3.2 / np.sqrt(C)
    blk = (np.random.uniform(0.0, 1.0, (K // BK, C // BN)) < KEEP).astype(np.float64)
    mask = np.repeat(np.repeat(blk, BK, axis=0), BN, axis=1)
    weight = weight * mask / s[None, :]
    bias = np.random.uniform(-1.0, 1.0, K) * 0.5
    return {"x": bf(x), "weight": bf(weight), "bias": bf(bias)}


def reference(x, weight, bias):
    return np.maximum((mxq(f64(x), 1, "e4m3") @ mxq(f64(weight), 1, "e4m3").T) + f64(bias), 0.0)

@@ -1,0 +1,186 @@
+from contextlib import ExitStack
+
+import concourse.mybir as mybir
+from concourse.masks import make_identity
+
+FLOPS = 2 * 16384 * 512 * 128
+
+BF16 = mybir.dt.bfloat16
+F32 = mybir.dt.float32
+U32 = mybir.dt.uint32
+U8 = mybir.dt.uint8
+FP8X4 = mybir.dt.float8_e4m3fn_x4
+ADD = mybir.AluOpType.add
+RELU = mybir.ActivationFunctionType.Relu
+
+P = 128
+K = 512
+KW = K // 2
+NF = 128
+UNIT = 4
+CHUNKS = (4, 4, 8, 16, 16, 16, 16, 16, 16, 16)
+LAST_STORES = (8, 4, 4)
+RELU_ON_SCALAR = (2, 5, 7)
+
+
+def tile_sparselinearrelu_t_kernel(tc, x, weight, bias, out):
+    nc = tc.nc
+    with ExitStack() as ctx:
+        const = ctx.enter_context(tc.tile_pool(name="const", bufs=1))
+        xpool = ctx.enter_context(tc.tile_pool(name="xres", bufs=1))
+        opool = ctx.enter_context(tc.tile_pool(name="ores", bufs=1))
+        work = ctx.enter_context(tc.tile_pool(name="work", bufs=3))
+        psum = ctx.enter_context(tc.psum_pool(name="psum", bufs=2))
+        ctx.enter_context(tc.manual_schedule())
+
+        w_sb = const.tile([P, K], BF16, name="w_sb")
+        nc.scalar.dma_start(out=w_sb[:], in_=weight)
+        brow = const.tile([P, 512], BF16, name="brow")
+        nc.vector.memset(brow[:], 0.0)
+        ones = const.tile([P, P], BF16, name="ones")
+        nc.vector.memset(ones[:], 1.0)
+        nc.scalar.dma_start(out=brow[0:1, 0:NF], in_=bias.rearrange("(o n) -> o n", o=1))
+        ident = const.tile([P, P], F32, name="ident")
+        make_identity(nc, ident[:])
+        warm = const.tile([P, 1], F32, name="warm")
+        nc.scalar.activation(out=warm[:], in_=ones[:, 0:1], func=RELU)
+
+        x_tiles = []
+        o_tiles = []
+        row0 = []
+        units = []
+        r = 0
+        for c, t_n in enumerate(CHUNKS):
+            xc = xpool.tile([P, t_n * K], BF16, name="x%d" % c)
+            nc.sync.dma_start(
+                out=xc[:], in_=x[r : r + P * t_n, :].rearrange("(p t) k -> p (t k)", t=t_n)
+            )
+            oc = opool.tile([P, t_n * NF], F32, name="o%d" % c)
+            x_tiles.append(xc)
+            o_tiles.append(oc)
+            row0.append(r)
+            r += P * t_n
+            for t0 in range(0, t_n, UNIT):
+                units.append((c, t0))
+        n_units = len(units)
+
+        banks = {}
+        grouped = {}
+        codes = {}
+        planes = {}
+        accs = {}
+
+        def regroup(dst_words, bank, n_tiles):
+            nc.scalar.copy(
+                out=dst_words.rearrange("p (a r s) -> p a r s", a=n_tiles, s=2),
+                in_=bank.rearrange("p (a s r) -> p a r s", a=n_tiles, s=2),
+            )
+
+        w_words = w_sb[:].bitcast(F32)
+        w_bank = psum.tile([P, 512], F32, name="w_bank", tag="xt", bufs=6)
+        for s in range(2):
+            nc.tensor.transpose(w_bank[:, s * P : (s + 1) * P], w_words[:, s * P : (s + 1) * P], ident[:])
+        w_grouped = const.tile([P, NF * 4], BF16, name="w_grouped", align_bytes=64)
+        regroup(w_grouped[:].bitcast(F32), w_bank[:, 0 : 2 * P], 1)
+        w_codes = const.tile([P, NF], U32, name="w_codes", align_bytes=64)
+        w_plane = const.tile([P, NF], U8, name="w_plane", align_bytes=64)
+        nc.vector.quantize_mx(out=w_codes[:].bitcast(FP8X4), scales=w_plane[:], in_=w_grouped[:])
+
+        bias4 = const.tile([P, UNIT * NF], F32, name="bias4")
+
+        def spread_bias():
+            b_bank = psum.tile([P, 512], F32, name="b_bank", tag="acc", bufs=2)
+            nc.tensor.matmul(b_bank[:], lhsT=ones[:], rhs=brow[:], start=True, stop=True)
+            for a in range(UNIT):
+                nc.vector.tensor_copy(out=bias4[:, a * NF : (a + 1) * NF], in_=b_bank[:, 0:NF])
+
+        def transposes(u):
+            c, t0 = units[u]
+            words = x_tiles[c][:].bitcast(F32)
+            pair = []
+            for h in range(2):
+                bank = psum.tile([P, 512], F32, name="xt%d_%d" % (u, h), tag="xt", bufs=6)
+                for j in range(4):
+                    col = (t0 + 2 * h) * KW + j * P
+                    nc.tensor.transpose(bank[:, j * P : (j + 1) * P], words[:, col : col + P], ident[:])
+                pair.append(bank)
+            banks[u] = pair
+
+        def evacuate(u):
+            g = work.tile([P, UNIT * K], BF16, name="g%d" % u, tag="grouped", align_bytes=64)
+            g_words = g[:].bitcast(F32)
+            for h in range(2):
+                regroup(g_words[:, h * 512 : (h + 1) * 512], banks[u][h][:], 2)
+            grouped[u] = g
+
+        def quantise(u):
+            cw = work.tile([P, UNIT * P], U32, name="c%d" % u, tag="codes", align_bytes=64)
+            pl = work.tile([P, UNIT * P], U8, name="s%d" % u, tag="plane", align_bytes=64)
+            nc.vector.quantize_mx(out=cw[:].bitcast(FP8X4), scales=pl[:], in_=grouped[u][:])
+            codes[u] = cw
+            planes[u] = pl
+
+        def multiply(u):
+            acc = psum.tile([P, UNIT * NF], F32, name="acc%d" % u, tag="acc", bufs=2)
+            for a in range(UNIT):
+                cols = slice(a * P, (a + 1) * P)
+                nc.tensor.matmul_mx(
+                    out=acc[:, a * NF : (a + 1) * NF],
+                    lhsT=codes[u][:, cols].bitcast(FP8X4),
+                    lhsT_scale=planes[u][:, cols],
+                    rhs=w_codes[:].bitcast(FP8X4),
+                    rhs_scale=w_plane[:],
+                    start=True,
+                    stop=True,
+                )
+            accs[u] = acc
+
+        def o_slice(u):
+            c, t0 = units[u]
+            return o_tiles[c][:, t0 * NF : (t0 + UNIT) * NF]
+
+        def add_bias(u):
+            nc.vector.tensor_tensor(out=o_slice(u), in0=accs[u][:], in1=bias4[:], op=ADD)
+
+        def relu(u):
+            if u % 8 in RELU_ON_SCALAR:
+                nc.scalar.activation(out=o_slice(u), in_=o_slice(u), func=RELU)
+            else:
+                nc.vector.tensor_scalar_max(out=o_slice(u), in0=o_slice(u), scalar1=0.0)
+
+        stores = {}
+        u = 0
+        for c, t_n in enumerate(CHUNKS):
+            parts = LAST_STORES if c == len(CHUNKS) - 1 else (t_n,)
+            t0 = 0
+            for n in parts:
+                u += n // UNIT
+                stores[u - 1] = (c, t0, n)
+                t0 += n
+
+        def store(u):
+            if u in stores:
+                c, t0, n = stores[u]
+                t_n = CHUNKS[c]
+                view = out[row0[c] : row0[c] + P * t_n, :].rearrange("(p t) f -> p t f", t=t_n)
+                nc.sync.dma_start(
+                    out=view[:, t0 : t0 + n, :],
+                    in_=o_tiles[c][:, t0 * NF : (t0 + n) * NF].rearrange("p (t f) -> p t f", f=NF),
+                )
+
+        for i in range(n_units + 5):
+            if i < n_units:
+                transposes(i)
+            if i == 2:
+                spread_bias()
+            if 0 <= i - 1 < n_units:
+                evacuate(i - 1)
+            if 0 <= i - 2 < n_units:
+                quantise(i - 2)
+            if 0 <= i - 3 < n_units:
+                multiply(i - 3)
+            if 0 <= i - 4 < n_units:
+                add_bias(i - 4)
+            if 0 <= i - 5 < n_units:
+                relu(i - 5)
+                store(i - 5)

@@ -20,7 +20,7 @@ NF = 128
 UNIT = 4
 CHUNKS = (4, 4, 8, 16, 16, 16, 16, 16, 16, 16)
 LAST_STORES = (8, 4, 4)
-RELU_ON_SCALAR = (2, 5, 7)
+RELU_V = 320
 
 
 def tile_sparselinearrelu_t_kernel(tc, x, weight, bias, out):
@@ -29,7 +29,7 @@ def tile_sparselinearrelu_t_kernel(tc, x, weight, bias, out):
         const = ctx.enter_context(tc.tile_pool(name="const", bufs=1))
         xpool = ctx.enter_context(tc.tile_pool(name="xres", bufs=1))
         opool = ctx.enter_context(tc.tile_pool(name="ores", bufs=1))
-        work = ctx.enter_context(tc.tile_pool(name="work", bufs=3))
+        work = ctx.enter_context(tc.tile_pool(name="work", bufs=4))
         psum = ctx.enter_context(tc.psum_pool(name="psum", bufs=2))
         ctx.enter_context(tc.manual_schedule())
 
@@ -143,10 +143,10 @@ def tile_sparselinearrelu_t_kernel(tc, x, weight, bias, out):
             nc.vector.tensor_tensor(out=o_slice(u), in0=accs[u][:], in1=bias4[:], op=ADD)
 
         def relu(u):
-            if u % 8 in RELU_ON_SCALAR:
-                nc.scalar.activation(out=o_slice(u), in_=o_slice(u), func=RELU)
-            else:
-                nc.vector.tensor_scalar_max(out=o_slice(u), in0=o_slice(u), scalar1=0.0)
+            o_v = o_slice(u)[:, 0:RELU_V]
+            o_s = o_slice(u)[:, RELU_V : UNIT * NF]
+            nc.vector.tensor_scalar_max(out=o_v, in0=o_v, scalar1=0.0)
+            nc.scalar.activation(out=o_s, in_=o_s, func=RELU)
 
         stores = {}
         u = 0

@@ -18,9 +18,10 @@ K = 512
 KW = K // 2
 NF = 128
 UNIT = 4
-CHUNKS = (4, 4, 8, 16, 16, 16, 16, 16, 16, 16)
-LAST_STORES = (8, 4, 4)
-RELU_V = 320
+GROUP = 32
+LOADS = ((2, 2, 4, 4, 4, 4, 4, 8), (8, 8, 8, 8), (12, 12, 8), (16, 16))
+STORES = ((32,), (32,), (32,), (16, 8, 4, 2, 2))
+RELU_V = 80
 
 
 def tile_sparselinearrelu_t_kernel(tc, x, weight, bias, out):
@@ -45,23 +46,34 @@ def tile_sparselinearrelu_t_kernel(tc, x, weight, bias, out):
         warm = const.tile([P, 1], F32, name="warm")
         nc.scalar.activation(out=warm[:], in_=ones[:, 0:1], func=RELU)
 
-        x_tiles = []
-        o_tiles = []
-        row0 = []
         units = []
-        r = 0
-        for c, t_n in enumerate(CHUNKS):
-            xc = xpool.tile([P, t_n * K], BF16, name="x%d" % c)
-            nc.sync.dma_start(
-                out=xc[:], in_=x[r : r + P * t_n, :].rearrange("(p t) k -> p (t k)", t=t_n)
-            )
-            oc = opool.tile([P, t_n * NF], F32, name="o%d" % c)
-            x_tiles.append(xc)
-            o_tiles.append(oc)
-            row0.append(r)
-            r += P * t_n
-            for t0 in range(0, t_n, UNIT):
-                units.append((c, t0))
+        stores = {}
+        for g in range(len(LOADS)):
+            rows = slice(g * GROUP * P, (g + 1) * GROUP * P)
+            x_view = x[rows, :].rearrange("(p t) k -> p t k", t=GROUP)
+            o_view = out[rows, :].rearrange("(p t) f -> p t f", t=GROUP)
+            x_of = []
+            t0 = 0
+            for n in LOADS[g]:
+                xc = xpool.tile([P, n * K], BF16, name="x%d_%d" % (g, t0))
+                nc.sync.dma_start(
+                    out=xc[:].rearrange("p (t k) -> p t k", k=K), in_=x_view[:, t0 : t0 + n, :]
+                )
+                for j in range(n):
+                    x_of.append((xc, j, n - j))
+                t0 += n
+            t0 = 0
+            for n in STORES[g]:
+                oc = opool.tile([P, n * NF], F32, name="o%d_%d" % (g, t0))
+                nxt = 0
+                for j in range(n):
+                    if j == nxt:
+                        xc, xj, left = x_of[t0 + j]
+                        size = min(UNIT, left, n - j)
+                        units.append((xc, xj, oc, j, size))
+                        nxt = j + size
+                stores[len(units) - 1] = (o_view[:, t0 : t0 + n, :], oc)
+                t0 += n
         n_units = len(units)
 
         banks = {}
@@ -95,34 +107,39 @@ def tile_sparselinearrelu_t_kernel(tc, x, weight, bias, out):
                 nc.vector.tensor_copy(out=bias4[:, a * NF : (a + 1) * NF], in_=b_bank[:, 0:NF])
 
         def transposes(u):
-            c, t0 = units[u]
-            words = x_tiles[c][:].bitcast(F32)
-            pair = []
-            for h in range(2):
+            xc, xj, oc, oj, size = units[u]
+            words = xc[:].bitcast(F32)
+            made = []
+            for h in range(size // 2):
                 bank = psum.tile([P, 512], F32, name="xt%d_%d" % (u, h), tag="xt", bufs=6)
                 for j in range(4):
-                    col = (t0 + 2 * h) * KW + j * P
+                    col = (xj + 2 * h) * KW + j * P
                     nc.tensor.transpose(bank[:, j * P : (j + 1) * P], words[:, col : col + P], ident[:])
-                pair.append(bank)
-            banks[u] = pair
+                made.append(bank)
+            banks[u] = made
 
         def evacuate(u):
             g = work.tile([P, UNIT * K], BF16, name="g%d" % u, tag="grouped", align_bytes=64)
             g_words = g[:].bitcast(F32)
-            for h in range(2):
+            for h in range(len(banks[u])):
                 regroup(g_words[:, h * 512 : (h + 1) * 512], banks[u][h][:], 2)
             grouped[u] = g
 
         def quantise(u):
+            size = units[u][4]
             cw = work.tile([P, UNIT * P], U32, name="c%d" % u, tag="codes", align_bytes=64)
             pl = work.tile([P, UNIT * P], U8, name="s%d" % u, tag="plane", align_bytes=64)
-            nc.vector.quantize_mx(out=cw[:].bitcast(FP8X4), scales=pl[:], in_=grouped[u][:])
+            nc.vector.quantize_mx(
+                out=cw[:, 0 : size * P].bitcast(FP8X4),
+                scales=pl[:, 0 : size * P],
+                in_=grouped[u][:, 0 : size * K],
+            )
             codes[u] = cw
             planes[u] = pl
 
         def multiply(u):
             acc = psum.tile([P, UNIT * NF], F32, name="acc%d" % u, tag="acc", bufs=2)
-            for a in range(UNIT):
+            for a in range(units[u][4]):
                 cols = slice(a * P, (a + 1) * P)
                 nc.tensor.matmul_mx(
                     out=acc[:, a * NF : (a + 1) * NF],
@@ -135,38 +152,27 @@ def tile_sparselinearrelu_t_kernel(tc, x, weight, bias, out):
                 )
             accs[u] = acc
 
-        def o_slice(u):
-            c, t0 = units[u]
-            return o_tiles[c][:, t0 * NF : (t0 + UNIT) * NF]
-
         def add_bias(u):
-            nc.vector.tensor_tensor(out=o_slice(u), in0=accs[u][:], in1=bias4[:], op=ADD)
+            xc, xj, oc, oj, size = units[u]
+            nc.vector.tensor_tensor(
+                out=oc[:, oj * NF : (oj + size) * NF],
+                in0=accs[u][:, 0 : size * NF],
+                in1=bias4[:, 0 : size * NF],
+                op=ADD,
+            )
 
         def relu(u):
-            o_v = o_slice(u)[:, 0:RELU_V]
-            o_s = o_slice(u)[:, RELU_V : UNIT * NF]
+            xc, xj, oc, oj, size = units[u]
+            cut = oj * NF + size * RELU_V
+            o_v = oc[:, oj * NF : cut]
+            o_s = oc[:, cut : (oj + size) * NF]
             nc.vector.tensor_scalar_max(out=o_v, in0=o_v, scalar1=0.0)
             nc.scalar.activation(out=o_s, in_=o_s, func=RELU)
 
-        stores = {}
-        u = 0
-        for c, t_n in enumerate(CHUNKS):
-            parts = LAST_STORES if c == len(CHUNKS) - 1 else (t_n,)
-            t0 = 0
-            for n in parts:
-                u += n // UNIT
-                stores[u - 1] = (c, t0, n)
-                t0 += n
-
         def store(u):
             if u in stores:
-                c, t0, n = stores[u]
-                t_n = CHUNKS[c]
-                view = out[row0[c] : row0[c] + P * t_n, :].rearrange("(p t) f -> p t f", t=t_n)
-                nc.sync.dma_start(
-                    out=view[:, t0 : t0 + n, :],
-                    in_=o_tiles[c][:, t0 * NF : (t0 + n) * NF].rearrange("p (t f) -> p t f", f=NF),
-                )
+                view, oc = stores[u]
+                nc.sync.dma_start(out=view, in_=oc[:].rearrange("p (t f) -> p t f", f=NF))
 
         for i in range(n_units + 5):
             if i < n_units:

@@ -11,6 +11,9 @@ U32 = mybir.dt.uint32
 U8 = mybir.dt.uint8
 FP8X4 = mybir.dt.float8_e4m3fn_x4
 ADD = mybir.AluOpType.add
+MIN = mybir.AluOpType.min
+MAX = mybir.AluOpType.max
+F32_MAX = 3.4028234663852886e38
 RELU = mybir.ActivationFunctionType.Relu
 
 P = 128
@@ -18,10 +21,12 @@ K = 512
 KW = K // 2
 NF = 128
 UNIT = 4
-GROUP = 32
-LOADS = ((2, 2, 4, 4, 4, 4, 4, 8), (8, 8, 8, 8), (12, 12, 8), (16, 16))
-STORES = ((32,), (32,), (32,), (16, 8, 4, 2, 2))
-RELU_V = 80
+LOADS = ((2, 4, 4, 6, 8, 8), (12, 16, 20), (24, 24))
+STORES = ((32,), (48,), (24, 12, 6, 4, 2))
+RELU_SPLIT = (40, 24, 64)
+RELU_SPLIT_END = (80, 48, 0)
+END_UNITS = 3
+WARM_UP = 4
 
 
 def tile_sparselinearrelu_t_kernel(tc, x, weight, bias, out):
@@ -36,10 +41,15 @@ def tile_sparselinearrelu_t_kernel(tc, x, weight, bias, out):
 
         w_sb = const.tile([P, K], BF16, name="w_sb")
         nc.scalar.dma_start(out=w_sb[:], in_=weight)
-        brow = const.tile([P, 512], BF16, name="brow")
-        nc.vector.memset(brow[:], 0.0)
         ones = const.tile([P, P], BF16, name="ones")
         nc.vector.memset(ones[:], 1.0)
+        zeros = const.tile([P, 512], BF16, name="zeros")
+        nc.vector.memset(zeros[:], 0.0)
+        brow = const.tile([P, 512], BF16, name="brow")
+        nc.vector.memset(brow[:], 0.0)
+        warm_bank = psum.tile([P, 512], F32, name="warm_bank", tag="acc", bufs=2)
+        for k in range(WARM_UP):
+            nc.tensor.matmul(warm_bank[:], lhsT=ones[:], rhs=zeros[:], start=True, stop=True)
         nc.scalar.dma_start(out=brow[0:1, 0:NF], in_=bias.rearrange("(o n) -> o n", o=1))
         ident = const.tile([P, P], F32, name="ident")
         make_identity(nc, ident[:])
@@ -48,10 +58,13 @@ def tile_sparselinearrelu_t_kernel(tc, x, weight, bias, out):
 
         units = []
         stores = {}
+        base = 0
         for g in range(len(LOADS)):
-            rows = slice(g * GROUP * P, (g + 1) * GROUP * P)
-            x_view = x[rows, :].rearrange("(p t) k -> p t k", t=GROUP)
-            o_view = out[rows, :].rearrange("(p t) f -> p t f", t=GROUP)
+            t_g = sum(LOADS[g])
+            rows = slice(base, base + t_g * P)
+            base += t_g * P
+            x_view = x[rows, :].rearrange("(p t) k -> p t k", t=t_g)
+            o_view = out[rows, :].rearrange("(p t) f -> p t f", t=t_g)
             x_of = []
             t0 = 0
             for n in LOADS[g]:
@@ -163,11 +176,17 @@ def tile_sparselinearrelu_t_kernel(tc, x, weight, bias, out):
 
         def relu(u):
             xc, xj, oc, oj, size = units[u]
-            cut = oj * NF + size * RELU_V
-            o_v = oc[:, oj * NF : cut]
-            o_s = oc[:, cut : (oj + size) * NF]
-            nc.vector.tensor_scalar_max(out=o_v, in0=o_v, scalar1=0.0)
-            nc.scalar.activation(out=o_s, in_=o_s, func=RELU)
+            n_v, n_s, n_g = RELU_SPLIT if u < n_units - END_UNITS else RELU_SPLIT_END
+            c0 = oj * NF
+            c1 = c0 + size * n_v
+            c2 = c1 + size * n_s
+            c3 = c2 + size * n_g
+            nc.vector.tensor_scalar_max(out=oc[:, c0:c1], in0=oc[:, c0:c1], scalar1=0.0)
+            nc.scalar.activation(out=oc[:, c1:c2], in_=oc[:, c1:c2], func=RELU)
+            if n_g:
+                nc.gpsimd.tensor_scalar(
+                    out=oc[:, c2:c3], in0=oc[:, c2:c3], scalar1=F32_MAX, scalar2=0.0, op0=MIN, op1=MAX
+                )
 
         def store(u):
             if u in stores:

@@ -39,18 +39,18 @@ def tile_sparselinearrelu_t_kernel(tc, x, weight, bias, out):
         psum = ctx.enter_context(tc.psum_pool(name="psum", bufs=2))
         ctx.enter_context(tc.manual_schedule())
 
+        brow = const.tile([P, NF], BF16, name="brow")
+        nc.vector.memset(brow[:], 0.0)
+        nc.scalar.dma_start(out=brow[0:1, :], in_=bias.rearrange("(o n) -> o n", o=1))
         w_sb = const.tile([P, K], BF16, name="w_sb")
         nc.scalar.dma_start(out=w_sb[:], in_=weight)
         ones = const.tile([P, P], BF16, name="ones")
         nc.vector.memset(ones[:], 1.0)
         zeros = const.tile([P, 512], BF16, name="zeros")
         nc.vector.memset(zeros[:], 0.0)
-        brow = const.tile([P, 512], BF16, name="brow")
-        nc.vector.memset(brow[:], 0.0)
         warm_bank = psum.tile([P, 512], F32, name="warm_bank", tag="acc", bufs=2)
         for k in range(WARM_UP):
             nc.tensor.matmul(warm_bank[:], lhsT=ones[:], rhs=zeros[:], start=True, stop=True)
-        nc.scalar.dma_start(out=brow[0:1, 0:NF], in_=bias.rearrange("(o n) -> o n", o=1))
         ident = const.tile([P, P], F32, name="ident")
         make_identity(nc, ident[:])
         warm = const.tile([P, 1], F32, name="warm")
@@ -115,7 +115,7 @@ def tile_sparselinearrelu_t_kernel(tc, x, weight, bias, out):
 
         def spread_bias():
             b_bank = psum.tile([P, 512], F32, name="b_bank", tag="acc", bufs=2)
-            nc.tensor.matmul(b_bank[:], lhsT=ones[:], rhs=brow[:], start=True, stop=True)
+            nc.tensor.matmul(b_bank[:, 0:NF], lhsT=ones[:], rhs=brow[:], start=True, stop=True)
             for a in range(UNIT):
                 nc.vector.tensor_copy(out=bias4[:, a * NF : (a + 1) * NF], in_=b_bank[:, 0:NF])
 

@@ -23,7 +23,7 @@ NF = 128
 UNIT = 4
 LOADS = ((2, 4, 4, 6, 8, 8), (12, 16, 20), (24, 24))
 STORES = ((32,), (48,), (24, 12, 6, 4, 2))
-RELU_SPLIT = (40, 24, 64)
+RELU_SPLIT = (0, 32, 96)
 RELU_SPLIT_END = (80, 48, 0)
 END_UNITS = 3
 WARM_UP = 4
@@ -181,7 +181,8 @@ def tile_sparselinearrelu_t_kernel(tc, x, weight, bias, out):
             c1 = c0 + size * n_v
             c2 = c1 + size * n_s
             c3 = c2 + size * n_g
-            nc.vector.tensor_scalar_max(out=oc[:, c0:c1], in0=oc[:, c0:c1], scalar1=0.0)
+            if n_v:
+                nc.vector.tensor_scalar_max(out=oc[:, c0:c1], in0=oc[:, c0:c1], scalar1=0.0)
             nc.scalar.activation(out=oc[:, c1:c2], in_=oc[:, c1:c2], func=RELU)
             if n_g:
                 nc.gpsimd.tensor_scalar(

@@ -194,19 +194,25 @@ def tile_sparselinearrelu_t_kernel(tc, x, weight, bias, out):
                 view, oc = stores[u]
                 nc.sync.dma_start(out=view, in_=oc[:].rearrange("p (t f) -> p t f", f=NF))
 
-        for i in range(n_units + 5):
-            if i < n_units:
-                transposes(i)
+        stage_order = (
+            (transposes, 0),
+            (transposes, 1),
+            (add_bias, -5),
+            (evacuate, -1),
+            (relu, -6),
+            (store, -6),
+            (quantise, -2),
+            (add_bias, -4),
+            (evacuate, 0),
+            (relu, -5),
+            (store, -5),
+            (quantise, -1),
+            (multiply, -3),
+            (multiply, -2),
+        )
+        for i in range(0, n_units + 7, 2):
             if i == 2:
                 spread_bias()
-            if 0 <= i - 1 < n_units:
-                evacuate(i - 1)
-            if 0 <= i - 2 < n_units:
-                quantise(i - 2)
-            if 0 <= i - 3 < n_units:
-                multiply(i - 3)
-            if 0 <= i - 4 < n_units:
-                add_bias(i - 4)
-            if 0 <= i - 5 < n_units:
-                relu(i - 5)
-                store(i - 5)
+            for stage, lag in stage_order:
+                if 0 <= i + lag < n_units:
+                    stage(i + lag)

@@ -22,7 +22,7 @@ KW = K // 2
 NF = 128
 UNIT = 4
 LOADS = ((2, 4, 4, 6, 8, 8), (12, 16, 20), (24, 24))
-STORES = ((32,), (48,), (24, 12, 6, 4, 2))
+STORES = ((16, 16), (16, 16, 16), (16, 12, 10, 6, 4))
 RELU_SPLIT = (0, 32, 96)
 RELU_SPLIT_END = (80, 48, 0)
 END_UNITS = 3
@@ -41,9 +41,9 @@ def tile_sparselinearrelu_t_kernel(tc, x, weight, bias, out):
 
         brow = const.tile([P, NF], BF16, name="brow")
         nc.vector.memset(brow[:], 0.0)
-        nc.scalar.dma_start(out=brow[0:1, :], in_=bias.rearrange("(o n) -> o n", o=1))
         w_sb = const.tile([P, K], BF16, name="w_sb")
         nc.scalar.dma_start(out=w_sb[:], in_=weight)
+        nc.scalar.dma_start(out=brow[0:1, :], in_=bias.rearrange("(o n) -> o n", o=1))
         ones = const.tile([P, P], BF16, name="ones")
         nc.vector.memset(ones[:], 1.0)
         zeros = const.tile([P, 512], BF16, name="zeros")
@@ -211,7 +211,7 @@ def tile_sparselinearrelu_t_kernel(tc, x, weight, bias, out):
             (multiply, -2),
         )
         for i in range(0, n_units + 7, 2):
-            if i == 2:
+            if i == 4:
                 spread_bias()
             for stage, lag in stage_order:
                 if 0 <= i + lag < n_units:

@@ -21,8 +21,8 @@ K = 512
 KW = K // 2
 NF = 128
 UNIT = 4
-LOADS = ((2, 4, 4, 6, 8, 8), (12, 16, 20), (24, 24))
-STORES = ((16, 16), (16, 16, 16), (16, 12, 10, 6, 4))
+LOADS = ((2, 2, 4, 8, 16), (16, 16), (16, 16), (16, 16))
+STORES = ((16, 16), (16, 16), (16, 16), (16, 8, 4, 4))
 RELU_SPLIT = (0, 32, 96)
 RELU_SPLIT_END = (80, 48, 0)
 END_UNITS = 3

@@ -41,8 +41,8 @@ def tile_sparselinearrelu_t_kernel(tc, x, weight, bias, out):
 
         brow = const.tile([P, NF], BF16, name="brow")
         nc.vector.memset(brow[:], 0.0)
-        w_sb = const.tile([P, K], BF16, name="w_sb")
-        nc.scalar.dma_start(out=w_sb[:], in_=weight)
+        w_sb = const.tile([P, K], BF16, name="w_sb", align_bytes=512)
+        nc.sync.dma_start(out=w_sb[:], in_=weight)
         nc.scalar.dma_start(out=brow[0:1, :], in_=bias.rearrange("(o n) -> o n", o=1))
         ones = const.tile([P, P], BF16, name="ones")
         nc.vector.memset(ones[:], 1.0)
@@ -68,7 +68,7 @@ def tile_sparselinearrelu_t_kernel(tc, x, weight, bias, out):
             x_of = []
             t0 = 0
             for n in LOADS[g]:
-                xc = xpool.tile([P, n * K], BF16, name="x%d_%d" % (g, t0))
+                xc = xpool.tile([P, n * K], BF16, name="x%d_%d" % (g, t0), align_bytes=512)
                 nc.sync.dma_start(
                     out=xc[:].rearrange("p (t k) -> p t k", k=K), in_=x_view[:, t0 : t0 + n, :]
                 )
@@ -77,7 +77,7 @@ def tile_sparselinearrelu_t_kernel(tc, x, weight, bias, out):
                 t0 += n
             t0 = 0
             for n in STORES[g]:
-                oc = opool.tile([P, n * NF], F32, name="o%d_%d" % (g, t0))
+                oc = opool.tile([P, n * NF], F32, name="o%d_%d" % (g, t0), align_bytes=512)
                 nxt = 0
                 for j in range(n):
                     if j == nxt:

from contextlib import ExitStack

import concourse.mybir as mybir
from concourse.masks import make_identity

FLOPS = 2 * 16384 * 512 * 128

BF16 = mybir.dt.bfloat16
F32 = mybir.dt.float32
U32 = mybir.dt.uint32
U8 = mybir.dt.uint8
FP8X4 = mybir.dt.float8_e4m3fn_x4
ADD = mybir.AluOpType.add
MIN = mybir.AluOpType.min
MAX = mybir.AluOpType.max
F32_MAX = 3.4028234663852886e38
RELU = mybir.ActivationFunctionType.Relu

P = 128
K = 512
KW = K // 2
NF = 128
UNIT = 4
LOADS = ((2, 2, 4, 8, 16), (16, 16), (16, 16), (16, 16))
STORES = ((16, 16), (16, 16), (16, 16), (16, 8, 4, 4))
RELU_SPLIT = (0, 32, 96)
RELU_SPLIT_END = (80, 48, 0)
END_UNITS = 3
WARM_UP = 4


def tile_sparselinearrelu_t_kernel(tc, x, weight, bias, out):
    nc = tc.nc
    with ExitStack() as ctx:
        const = ctx.enter_context(tc.tile_pool(name="const", bufs=1))
        xpool = ctx.enter_context(tc.tile_pool(name="xres", bufs=1))
        opool = ctx.enter_context(tc.tile_pool(name="ores", bufs=1))
        work = ctx.enter_context(tc.tile_pool(name="work", bufs=4))
        psum = ctx.enter_context(tc.psum_pool(name="psum", bufs=2))
        ctx.enter_context(tc.manual_schedule())

        brow = const.tile([P, NF], BF16, name="brow")
        nc.vector.memset(brow[:], 0.0)
        w_sb = const.tile([P, K], BF16, name="w_sb", align_bytes=512)
        nc.sync.dma_start(out=w_sb[:], in_=weight)
        nc.scalar.dma_start(out=brow[0:1, :], in_=bias.rearrange("(o n) -> o n", o=1))
        ones = const.tile([P, P], BF16, name="ones")
        nc.vector.memset(ones[:], 1.0)
        zeros = const.tile([P, 512], BF16, name="zeros")
        nc.vector.memset(zeros[:], 0.0)
        warm_bank = psum.tile([P, 512], F32, name="warm_bank", tag="acc", bufs=2)
        for k in range(WARM_UP):
            nc.tensor.matmul(warm_bank[:], lhsT=ones[:], rhs=zeros[:], start=True, stop=True)
        ident = const.tile([P, P], F32, name="ident")
        make_identity(nc, ident[:])
        warm = const.tile([P, 1], F32, name="warm")
        nc.scalar.activation(out=warm[:], in_=ones[:, 0:1], func=RELU)

        units = []
        stores = {}
        base = 0
        for g in range(len(LOADS)):
            t_g = sum(LOADS[g])
            rows = slice(base, base + t_g * P)
            base += t_g * P
            x_view = x[rows, :].rearrange("(p t) k -> p t k", t=t_g)
            o_view = out[rows, :].rearrange("(p t) f -> p t f", t=t_g)
            x_of = []
            t0 = 0
            for n in LOADS[g]:
                xc = xpool.tile([P, n * K], BF16, name="x%d_%d" % (g, t0), align_bytes=512)
                nc.sync.dma_start(
                    out=xc[:].rearrange("p (t k) -> p t k", k=K), in_=x_view[:, t0 : t0 + n, :]
                )
                for j in range(n):
                    x_of.append((xc, j, n - j))
                t0 += n
            t0 = 0
            for n in STORES[g]:
                oc = opool.tile([P, n * NF], F32, name="o%d_%d" % (g, t0), align_bytes=512)
                nxt = 0
                for j in range(n):
                    if j == nxt:
                        xc, xj, left = x_of[t0 + j]
                        size = min(UNIT, left, n - j)
                        units.append((xc, xj, oc, j, size))
                        nxt = j + size
                stores[len(units) - 1] = (o_view[:, t0 : t0 + n, :], oc)
                t0 += n
        n_units = len(units)

        banks = {}
        grouped = {}
        codes = {}
        planes = {}
        accs = {}

        def regroup(dst_words, bank, n_tiles):
            nc.scalar.copy(
                out=dst_words.rearrange("p (a r s) -> p a r s", a=n_tiles, s=2),
                in_=bank.rearrange("p (a s r) -> p a r s", a=n_tiles, s=2),
            )

        w_words = w_sb[:].bitcast(F32)
        w_bank = psum.tile([P, 512], F32, name="w_bank", tag="xt", bufs=6)
        for s in range(2):
            nc.tensor.transpose(w_bank[:, s * P : (s + 1) * P], w_words[:, s * P : (s + 1) * P], ident[:])
        w_grouped = const.tile([P, NF * 4], BF16, name="w_grouped", align_bytes=64)
        regroup(w_grouped[:].bitcast(F32), w_bank[:, 0 : 2 * P], 1)
        w_codes = const.tile([P, NF], U32, name="w_codes", align_bytes=64)
        w_plane = const.tile([P, NF], U8, name="w_plane", align_bytes=64)
        nc.vector.quantize_mx(out=w_codes[:].bitcast(FP8X4), scales=w_plane[:], in_=w_grouped[:])

        bias4 = const.tile([P, UNIT * NF], F32, name="bias4")

        def spread_bias():
            b_bank = psum.tile([P, 512], F32, name="b_bank", tag="acc", bufs=2)
            nc.tensor.matmul(b_bank[:, 0:NF], lhsT=ones[:], rhs=brow[:], start=True, stop=True)
            for a in range(UNIT):
                nc.vector.tensor_copy(out=bias4[:, a * NF : (a + 1) * NF], in_=b_bank[:, 0:NF])

        def transposes(u):
            xc, xj, oc, oj, size = units[u]
            words = xc[:].bitcast(F32)
            made = []
            for h in range(size // 2):
                bank = psum.tile([P, 512], F32, name="xt%d_%d" % (u, h), tag="xt", bufs=6)
                for j in range(4):
                    col = (xj + 2 * h) * KW + j * P
                    nc.tensor.transpose(bank[:, j * P : (j + 1) * P], words[:, col : col + P], ident[:])
                made.append(bank)
            banks[u] = made

        def evacuate(u):
            g = work.tile([P, UNIT * K], BF16, name="g%d" % u, tag="grouped", align_bytes=64)
            g_words = g[:].bitcast(F32)
            for h in range(len(banks[u])):
                regroup(g_words[:, h * 512 : (h + 1) * 512], banks[u][h][:], 2)
            grouped[u] = g

        def quantise(u):
            size = units[u][4]
            cw = work.tile([P, UNIT * P], U32, name="c%d" % u, tag="codes", align_bytes=64)
            pl = work.tile([P, UNIT * P], U8, name="s%d" % u, tag="plane", align_bytes=64)
            nc.vector.quantize_mx(
                out=cw[:, 0 : size * P].bitcast(FP8X4),
                scales=pl[:, 0 : size * P],
                in_=grouped[u][:, 0 : size * K],
            )
            codes[u] = cw
            planes[u] = pl

        def multiply(u):
            acc = psum.tile([P, UNIT * NF], F32, name="acc%d" % u, tag="acc", bufs=2)
            for a in range(units[u][4]):
                cols = slice(a * P, (a + 1) * P)
                nc.tensor.matmul_mx(
                    out=acc[:, a * NF : (a + 1) * NF],
                    lhsT=codes[u][:, cols].bitcast(FP8X4),
                    lhsT_scale=planes[u][:, cols],
                    rhs=w_codes[:].bitcast(FP8X4),
                    rhs_scale=w_plane[:],
                    start=True,
                    stop=True,
                )
            accs[u] = acc

        def add_bias(u):
            xc, xj, oc, oj, size = units[u]
            nc.vector.tensor_tensor(
                out=oc[:, oj * NF : (oj + size) * NF],
                in0=accs[u][:, 0 : size * NF],
                in1=bias4[:, 0 : size * NF],
                op=ADD,
            )

        def relu(u):
            xc, xj, oc, oj, size = units[u]
            n_v, n_s, n_g = RELU_SPLIT if u < n_units - END_UNITS else RELU_SPLIT_END
            c0 = oj * NF
            c1 = c0 + size * n_v
            c2 = c1 + size * n_s
            c3 = c2 + size * n_g
            if n_v:
                nc.vector.tensor_scalar_max(out=oc[:, c0:c1], in0=oc[:, c0:c1], scalar1=0.0)
            nc.scalar.activation(out=oc[:, c1:c2], in_=oc[:, c1:c2], func=RELU)
            if n_g:
                nc.gpsimd.tensor_scalar(
                    out=oc[:, c2:c3], in0=oc[:, c2:c3], scalar1=F32_MAX, scalar2=0.0, op0=MIN, op1=MAX
                )

        def store(u):
            if u in stores:
                view, oc = stores[u]
                nc.sync.dma_start(out=view, in_=oc[:].rearrange("p (t f) -> p t f", f=NF))

        stage_order = (
            (transposes, 0),
            (transposes, 1),
            (add_bias, -5),
            (evacuate, -1),
            (relu, -6),
            (store, -6),
            (quantise, -2),
            (add_bias, -4),
            (evacuate, 0),
            (relu, -5),
            (store, -5),
            (quantise, -1),
            (multiply, -3),
            (multiply, -2),
        )
        for i in range(0, n_units + 7, 2):
            if i == 4:
                spread_bias()
            for stage, lag in stage_order:
                if 0 <= i + lag < n_units:
                    stage(i + lag)
